import numpy as np
import ml_dtypes


def mxq(x, axis, fmt="e4m3"):
    dtype, down = {"e4m3": (ml_dtypes.float8_e4m3fn, 7), "e5m2": (ml_dtypes.float8_e5m2, 14)}[fmt]
    v = np.moveaxis(np.asarray(x, np.float32).astype(ml_dtypes.bfloat16).astype(np.float64), axis, -1)
    blocks = v.reshape(v.shape[:-1] + (-1, 32))
    amax = np.abs(blocks).max(-1, keepdims=True)
    byte = np.maximum(np.where(amax > 0, np.frexp(amax)[1] - 1 + 127, 0) - down, 1)
    scale = np.exp2(byte - 127.0)
    codes = (blocks / scale).astype(np.float32).astype(dtype).astype(np.float64)
    return np.moveaxis((codes * scale).reshape(v.shape), -1, axis)


WIDE = False


def mx_kscale(k):
    if not WIDE:
        return np.ones(k)
    levels = np.array([10, -10, 5, -5, 0])
    a = np.random.permutation(np.resize(levels, k // 512 * 4)).reshape(k // 512, 4)
    idx = np.arange(k)
    return np.exp2(a[idx // 512, idx % 128 // 32])


BF16 = ml_dtypes.bfloat16


def bf(x):
    return np.asarray(x, np.float32).astype(BF16)


def f64(x):
    return np.asarray(x).astype(np.float64)


B, S, D, F, F2 = 4, 1024, 512, 512, 1024
EPS = 1e-6
D2 = 2 * D


def setup_inputs():
    n = np.random.standard_normal
    s, t = mx_kscale(F), mx_kscale(D2)
    tr, ti = t[:D], t[D:]
    wd = 1.5 / np.sqrt(F)
    return {'h_r': bf(n((B, S, F)) * 0.6 * s), 'h_i': bf(n((B, S, F)) * 0.6 * s),
            'w2r': bf(n((F, D)) * wd / s[:, None] * tr), 'b2r': bf(n(D) * 0.2 * tr),
            'w2i': bf(n((F, D)) * wd / s[:, None] * ti), 'b2i': bf(n(D) * 0.2 * ti),
            'We': bf(n((D2, D)) / np.sqrt(D2) / t[:, None]), 'be': bf(n(D) * 0.2),
            'g_rms': bf(1.0 + 0.1 * n(D))}


def reference(h_r, h_i, w2r, b2r, w2i, b2i, We, be, g_rms):
    rp = (mxq(f64(h_r), 2, 'e4m3') @ mxq(f64(w2r), 0, 'e4m3')) + f64(b2r)
    ip = (mxq(f64(h_i), 2, 'e4m3') @ mxq(f64(w2i), 0, 'e4m3')) + f64(b2i)
    cat = np.concatenate([rp, ip], axis=-1)
    wave = (mxq(cat, 2, 'e4m3') @ mxq(f64(We), 0, 'e4m3')) + f64(be)
    return wave * (1.0 / np.sqrt(np.mean(wave * wave, axis=-1, keepdims=True) + EPS)) * f64(g_rms)

@@ -1,0 +1,282 @@
+from contextlib import ExitStack
+
+import concourse.mybir as mybir
+from concourse.masks import make_identity
+
+F32 = mybir.dt.float32
+BF16 = mybir.dt.bfloat16
+U32 = mybir.dt.uint32
+U8 = mybir.dt.uint8
+FP8X4 = mybir.dt.float8_e4m3fn_x4
+ADD = mybir.AluOpType.add
+MULT = mybir.AluOpType.mult
+ACT = mybir.ActivationFunctionType
+
+P = 128
+PACK = 4
+TOKENS = 4096
+F = 512
+D = 512
+STREAMS = 2
+TILES = 2
+STEP_TOKENS = TILES * P
+STEPS = TOKENS // STEP_TOKENS
+PIECES = TILES * STREAMS
+EPS = 1e-6
+
+FLOPS = 2 * TOKENS * F * D * STREAMS + 2 * TOKENS * (STREAMS * D) * D
+
+
+def tile_wavenetworklm_pb_t_kernel(tc, h_r, h_i, w2r, b2r, w2i, b2i, We, be, g_rms, out):
+    nc = tc.nc
+    h_dram = [h_r.flatten_outer_dims(), h_i.flatten_outer_dims()]
+    w2_dram = [w2r, w2i]
+    b2_dram = [b2r, b2i]
+    out_dram = out.flatten_outer_dims()
+
+    with ExitStack() as stack:
+        stack.enter_context(tc.manual_schedule())
+        keep = stack.enter_context(tc.tile_pool(name="keep", bufs=1))
+        work = stack.enter_context(tc.tile_pool(name="work", bufs=2))
+        tail = stack.enter_context(tc.tile_pool(name="tail", bufs=3))
+        psum_t = stack.enter_context(tc.psum_pool(name="psum_t", bufs=2))
+        psum_1 = stack.enter_context(tc.psum_pool(name="psum_1", bufs=4))
+        psum_2 = stack.enter_context(tc.psum_pool(name="psum_2", bufs=2))
+
+        def load_h(n):
+            rows = slice(n * STEP_TOKENS, (n + 1) * STEP_TOKENS)
+            tiles = []
+            for s in range(STREAMS):
+                h_sb = keep.tile([P, TILES * F], BF16, name="h_%d_%d" % (s, n))
+                nc.sync.dma_start(out=h_sb[:], in_=h_dram[s][rows, :].rearrange("(p k) f -> p (k f)", k=TILES))
+                tiles.append(h_sb)
+            return tiles
+
+        def load_w2(s):
+            raw = keep.tile([P, PACK, D], BF16, name="w2_raw_%d" % s)
+            nc.sync.dma_start(
+                out=raw[:].rearrange("q (u e) d -> q u (e d)", u=2),
+                in_=w2_dram[s].rearrange("(u q e) d -> q u (e d)", u=2, e=2),
+            )
+            return raw
+
+        w2_raw = [None, None]
+        h_tiles = {}
+        w2_raw[0] = load_w2(0)
+        h_tiles[0] = load_h(0)
+        w2_raw[1] = load_w2(1)
+        h_tiles[1] = load_h(1)
+        we_raw = keep.tile([P, STREAMS, PACK, D], BF16)
+        nc.sync.dma_start(
+            out=we_raw[:].rearrange("p s t d -> p s (t d)"),
+            in_=We.rearrange("(s p t) d -> p s (t d)", s=STREAMS, t=PACK),
+        )
+        for n in range(2, STEPS):
+            h_tiles[n] = load_h(n)
+
+        identity = keep.tile([P, P], F32)
+        make_identity(nc, identity[:])
+        eps = keep.tile([P, 1], F32)
+        nc.vector.memset(eps[:], EPS)
+
+        b2 = []
+        for s in range(STREAMS):
+            b2_sb = keep.tile([P, PACK], BF16, name="b2_%d" % s)
+            nc.scalar.dma_start(out=b2_sb[:], in_=b2_dram[s].rearrange("(p t) -> p t", t=PACK))
+            b2.append(b2_sb)
+        be_all = keep.tile([P, D], BF16)
+        nc.gpsimd.dma_start(out=be_all[:], in_=be.partition_broadcast(P))
+        gain_all = keep.tile([P, D], BF16)
+        nc.gpsimd.dma_start(out=gain_all[:], in_=g_rms.partition_broadcast(P))
+
+        w2_codes = []
+        w2_scales = []
+
+        def prepare_w2(s):
+            grouped = keep.tile([P, D * PACK], BF16, name="w2_grouped_%d" % s, align_bytes=64)
+            nc.vector.tensor_copy(
+                out=grouped[:].rearrange("q (t c j) -> q t c j", t=PACK, j=PACK),
+                in_=w2_raw[s][:].rearrange("q j (c t) -> q t c j", t=PACK),
+            )
+            return grouped
+
+        def quantise_w2(s, grouped):
+            codes = keep.tile([P, D], U32, name="w2_codes_%d" % s, align_bytes=64)
+            scales = keep.tile([P, D], U8, name="w2_scales_%d" % s, align_bytes=64)
+            nc.vector.quantize_mx(out=codes[:].bitcast(FP8X4), scales=scales[:], in_=grouped[:])
+            w2_codes.append(codes)
+            w2_scales.append(scales)
+
+        w2_grouped = [prepare_w2(s) for s in range(STREAMS)]
+        for s in range(STREAMS):
+            quantise_w2(s, w2_grouped[s])
+
+        we_grouped = keep.tile([P, STREAMS, D * PACK], BF16, align_bytes=64)
+        we_codes = keep.tile([P, STREAMS, D], U32, align_bytes=64)
+        we_scales = keep.tile([P, STREAMS, D], U8, align_bytes=64)
+
+        def regroup_we():
+            nc.scalar.copy(
+                out=we_grouped[:, 0, :].rearrange("p (d t) -> p d t", t=PACK),
+                in_=we_raw[:, 0, :, :].rearrange("p t d -> p d t"),
+            )
+            nc.gpsimd.tensor_scalar(
+                out=we_grouped[:, 1, :].rearrange("p (d t) -> p d t", t=PACK),
+                in0=we_raw[:, 1, :, :].rearrange("p t d -> p d t"),
+                scalar1=1.0,
+                scalar2=0.0,
+                op0=MULT,
+                op1=ADD,
+            )
+
+        def quantise_we():
+            nc.vector.quantize_mx(
+                out=we_codes[:].rearrange("p s d -> p (s d)").bitcast(FP8X4),
+                scales=we_scales[:].rearrange("p s d -> p (s d)"),
+                in_=we_grouped[:].rearrange("p s x -> p (s x)"),
+            )
+
+        h_words = {}
+        h_grouped = {}
+        h_codes = {}
+        sums_1 = {}
+        cat_grouped = {}
+        cat_codes = {}
+        sums_2 = {}
+        gained = {}
+        inv_rms = {}
+
+        def transposes(n):
+            for k in range(TILES):
+                words = psum_t.tile([P, STREAMS, 2, P], F32)
+                for s in range(STREAMS):
+                    source = h_tiles[n][s][:].bitcast(F32)
+                    for u in range(2):
+                        first = k * (F // 2) + u * P
+                        nc.tensor.transpose(words[:, s, u, :], source[:, first : first + P], identity[:])
+                h_words[(n, k)] = words
+
+        def copy_h(n):
+            grouped = work.tile([P, PIECES * P * PACK], BF16, align_bytes=64)
+            grouped_words = grouped[:].bitcast(F32)
+            width = STREAMS * P * 2
+            for k in range(TILES):
+                nc.scalar.copy(
+                    out=grouped_words[:, k * width : (k + 1) * width].rearrange("p (s r u) -> p s r u", s=STREAMS, u=2),
+                    in_=h_words[(n, k)][:].rearrange("p s u r -> p s r u"),
+                )
+            h_grouped[n] = grouped
+
+        def quantise(grouped, codes_name, scales_name):
+            codes = work.tile([P, PIECES * P], U32, name=codes_name, align_bytes=64)
+            scales = work.tile([P, PIECES * P], U8, name=scales_name, align_bytes=64)
+            nc.vector.quantize_mx(out=codes[:].bitcast(FP8X4), scales=scales[:], in_=grouped[:])
+            return codes, scales
+
+        def quantise_h(n):
+            h_codes[n] = quantise(h_grouped[n], "h_codes", "h_scales")
+
+        def stage_1(n, piece):
+            s = piece % STREAMS
+            codes, scales = h_codes[n]
+            tokens = slice(piece * P, (piece + 1) * P)
+            sums = psum_1.tile([P, PACK, P], F32)
+            for t in range(PACK):
+                columns = slice(t * P, (t + 1) * P)
+                nc.tensor.matmul_mx(
+                    out=sums[:, t, :],
+                    lhsT=w2_codes[s][:, columns].bitcast(FP8X4),
+                    lhsT_scale=w2_scales[s][:, columns],
+                    rhs=codes[:, tokens].bitcast(FP8X4),
+                    rhs_scale=scales[:, tokens],
+                    start=True,
+                    stop=True,
+                )
+            sums_1[(n, piece)] = sums
+
+        def new_cat(n):
+            cat = work.tile([P, PIECES * P * PACK], BF16, align_bytes=64)
+            cat_grouped[n] = cat
+
+        def bias_and_round(n, piece):
+            s = piece % STREAMS
+            width = P * PACK
+            nc.vector.tensor_tensor(
+                out=cat_grouped[n][:, piece * width : (piece + 1) * width].rearrange("p (r t) -> p r t", t=PACK),
+                in0=sums_1[(n, piece)][:].rearrange("p t r -> p r t"),
+                in1=b2[s][:].unsqueeze(1).to_broadcast([P, P, PACK]),
+                op=ADD,
+            )
+
+        def quantise_cat(n):
+            cat_codes[n] = quantise(cat_grouped[n], "cat_codes", "cat_scales")
+
+        def stage_2(n, k):
+            codes, scales = cat_codes[n]
+            sums = psum_2.tile([P, D], F32)
+            for s in range(STREAMS):
+                tokens = slice((k * STREAMS + s) * P, (k * STREAMS + s + 1) * P)
+                nc.tensor.matmul_mx(
+                    out=sums[:],
+                    lhsT=codes[:, tokens].bitcast(FP8X4),
+                    lhsT_scale=scales[:, tokens],
+                    rhs=we_codes[:, s, :].bitcast(FP8X4),
+                    rhs_scale=we_scales[:, s, :],
+                    start=(s == 0),
+                    stop=(s == STREAMS - 1),
+                )
+            sums_2[(n, k)] = sums
+
+        def norm_first_half(n):
+            biased = tail.tile([P, TILES, D], F32)
+            with_gain = tail.tile([P, TILES, D], F32)
+            totals = tail.tile([P, TILES], F32)
+            for k in range(TILES):
+                nc.vector.tensor_tensor(out=biased[:, k, :], in0=sums_2[(n, k)][:], in1=be_all[:], op=ADD)
+                squares = work.tile([P, D], BF16)
+                nc.scalar.activation(out=squares[:], in_=biased[:, k, :], func=ACT.Square, accum_out=totals[:, k : k + 1])
+                nc.gpsimd.tensor_tensor(out=with_gain[:, k, :], in0=biased[:, k, :], in1=gain_all[:], op=MULT)
+            factors = tail.tile([P, TILES], F32)
+            nc.scalar.activation(out=factors[:], in_=totals[:], func=ACT.Abs_reciprocal_sqrt, scale=1.0 / D, bias=eps[:])
+            gained[n] = with_gain
+            inv_rms[n] = factors
+
+        def norm_second_half(n):
+            result = tail.tile([P, TILES, D], F32)
+            for k in range(TILES):
+                nc.scalar.activation(out=result[:, k, :], in_=gained[n][:, k, :], func=ACT.Copy, scale=inv_rms[n][:, k : k + 1])
+            rows = slice(n * STEP_TOKENS, (n + 1) * STEP_TOKENS)
+            nc.sync.dma_start(
+                out=out_dram[rows, :].rearrange("(p k) d -> p (k d)", k=TILES),
+                in_=result[:].rearrange("p k d -> p (k d)"),
+            )
+
+        def is_step(n):
+            return 0 <= n < STEPS
+
+        for i in range(-3, STEPS + 2):
+            if is_step(i + 1):
+                quantise_h(i + 1)
+            if is_step(i + 2):
+                copy_h(i + 2)
+            if is_step(i - 2):
+                norm_second_half(i - 2)
+            if is_step(i):
+                new_cat(i)
+            for piece in range(PIECES):
+                if is_step(i):
+                    bias_and_round(i, piece)
+                if is_step(i + 1):
+                    stage_1(i + 1, piece)
+            if is_step(i + 3):
+                transposes(i + 3)
+            if i == -1:
+                regroup_we()
+            if is_step(i - 1):
+                norm_first_half(i - 1)
+            if i == 0:
+                quantise_we()
+            if is_step(i):
+                quantise_cat(i)
+                for k in range(TILES):
+                    stage_2(i, k)

@@ -143,7 +143,9 @@ def tile_wavenetworklm_pb_t_kernel(tc, h_r, h_i, w2r, b2r, w2i, b2i, We, be, g_r
         cat_grouped = {}
         cat_codes = {}
         sums_2 = {}
+        wave = {}
         gained = {}
+        square_sums = {}
         inv_rms = {}
 
         def transposes(n):
@@ -227,18 +229,27 @@ def tile_wavenetworklm_pb_t_kernel(tc, h_r, h_i, w2r, b2r, w2i, b2i, We, be, g_r
                 )
             sums_2[(n, k)] = sums
 
-        def norm_first_half(n):
+        def new_norm(n):
             biased = tail.tile([P, TILES, D], F32)
             with_gain = tail.tile([P, TILES, D], F32)
             totals = tail.tile([P, TILES], F32)
-            for k in range(TILES):
-                nc.vector.tensor_tensor(out=biased[:, k, :], in0=sums_2[(n, k)][:], in1=be_all[:], op=ADD)
-                squares = work.tile([P, D], BF16)
-                nc.scalar.activation(out=squares[:], in_=biased[:, k, :], func=ACT.Square, accum_out=totals[:, k : k + 1])
-                nc.gpsimd.tensor_tensor(out=with_gain[:, k, :], in0=biased[:, k, :], in1=gain_all[:], op=MULT)
-            factors = tail.tile([P, TILES], F32)
-            nc.scalar.activation(out=factors[:], in_=totals[:], func=ACT.Abs_reciprocal_sqrt, scale=1.0 / D, bias=eps[:])
+            wave[n] = biased
             gained[n] = with_gain
+            square_sums[n] = totals
+
+        def norm_first_half(n, k):
+            nc.vector.tensor_tensor(out=wave[n][:, k, :], in0=sums_2[(n, k)][:], in1=be_all[:], op=ADD)
+            squares = work.tile([P, D], BF16)
+            nc.scalar.activation(
+                out=squares[:], in_=wave[n][:, k, :], func=ACT.Square, accum_out=square_sums[n][:, k : k + 1]
+            )
+            nc.gpsimd.tensor_tensor(out=gained[n][:, k, :], in0=wave[n][:, k, :], in1=gain_all[:], op=MULT)
+
+        def reciprocal_rms(n):
+            factors = tail.tile([P, TILES], F32)
+            nc.scalar.activation(
+                out=factors[:], in_=square_sums[n][:], func=ACT.Abs_reciprocal_sqrt, scale=1.0 / D, bias=eps[:]
+            )
             inv_rms[n] = factors
 
         def norm_second_half(n):
@@ -254,29 +265,33 @@ def tile_wavenetworklm_pb_t_kernel(tc, h_r, h_i, w2r, b2r, w2i, b2i, We, be, g_r
         def is_step(n):
             return 0 <= n < STEPS
 
-        for i in range(-3, STEPS + 2):
-            if is_step(i + 1):
-                quantise_h(i + 1)
+        for i in range(-3, STEPS + 3):
             if is_step(i + 2):
                 copy_h(i + 2)
+            if is_step(i - 3):
+                norm_second_half(i - 3)
             if is_step(i - 2):
-                norm_second_half(i - 2)
-            if is_step(i):
-                new_cat(i)
-            for piece in range(PIECES):
-                if is_step(i):
-                    bias_and_round(i, piece)
-                if is_step(i + 1):
-                    stage_1(i + 1, piece)
+                new_norm(i - 2)
+            for k in range(TILES):
+                if is_step(i - 2):
+                    norm_first_half(i - 2, k)
+                if is_step(i - 1):
+                    stage_2(i - 1, k)
+            if is_step(i - 2):
+                reciprocal_rms(i - 2)
             if is_step(i + 3):
                 transposes(i + 3)
             if i == -1:
                 regroup_we()
-            if is_step(i - 1):
-                norm_first_half(i - 1)
-            if i == 0:
-                quantise_we()
+            if is_step(i):
+                new_cat(i)
+                for piece in range(PIECES):
+                    bias_and_round(i, piece)
+            if is_step(i + 1):
+                quantise_h(i + 1)
+                for piece in range(PIECES):
+                    stage_1(i + 1, piece)
             if is_step(i):
                 quantise_cat(i)
-                for k in range(TILES):
-                    stage_2(i, k)
+            if i == 0:
+                quantise_we()

@@ -107,9 +107,8 @@ def tile_wavenetworklm_pb_t_kernel(tc, h_r, h_i, w2r, b2r, w2i, b2i, We, be, g_r
             w2_codes.append(codes)
             w2_scales.append(scales)
 
-        w2_grouped = [prepare_w2(s) for s in range(STREAMS)]
         for s in range(STREAMS):
-            quantise_w2(s, w2_grouped[s])
+            quantise_w2(s, prepare_w2(s))
 
         we_grouped = keep.tile([P, STREAMS, D * PACK], BF16, align_bytes=64)
         we_codes = keep.tile([P, STREAMS, D], U32, align_bytes=64)
@@ -243,7 +242,10 @@ def tile_wavenetworklm_pb_t_kernel(tc, h_r, h_i, w2r, b2r, w2i, b2i, We, be, g_r
             nc.scalar.activation(
                 out=squares[:], in_=wave[n][:, k, :], func=ACT.Square, accum_out=square_sums[n][:, k : k + 1]
             )
-            nc.gpsimd.tensor_tensor(out=gained[n][:, k, :], in0=wave[n][:, k, :], in1=gain_all[:], op=MULT)
+
+        def apply_gain(n, k):
+            gain_engine = nc.vector if n == STEPS - 1 else nc.gpsimd
+            gain_engine.tensor_tensor(out=gained[n][:, k, :], in0=wave[n][:, k, :], in1=gain_all[:], op=MULT)
 
         def reciprocal_rms(n):
             factors = tail.tile([P, TILES], F32)
@@ -254,20 +256,19 @@ def tile_wavenetworklm_pb_t_kernel(tc, h_r, h_i, w2r, b2r, w2i, b2i, We, be, g_r
 
         def norm_second_half(n):
             result = tail.tile([P, TILES, D], F32)
+            rows = out_dram[n * STEP_TOKENS : (n + 1) * STEP_TOKENS, :].rearrange("(p k) d -> p k d", k=TILES)
             for k in range(TILES):
                 nc.scalar.activation(out=result[:, k, :], in_=gained[n][:, k, :], func=ACT.Copy, scale=inv_rms[n][:, k : k + 1])
-            rows = slice(n * STEP_TOKENS, (n + 1) * STEP_TOKENS)
-            nc.sync.dma_start(
-                out=out_dram[rows, :].rearrange("(p k) d -> p (k d)", k=TILES),
-                in_=result[:].rearrange("p k d -> p (k d)"),
-            )
+                nc.sync.dma_start(out=rows[:, k, :], in_=result[:, k, :])
 
         def is_step(n):
             return 0 <= n < STEPS
 
-        for i in range(-3, STEPS + 3):
-            if is_step(i + 2):
-                copy_h(i + 2)
+        for i in range(-2, STEPS + 3):
+            if is_step(i + 1):
+                copy_h(i + 1)
+            if i == 0:
+                regroup_we()
             if is_step(i - 3):
                 norm_second_half(i - 3)
             if is_step(i - 2):
@@ -278,11 +279,11 @@ def tile_wavenetworklm_pb_t_kernel(tc, h_r, h_i, w2r, b2r, w2i, b2i, We, be, g_r
                 if is_step(i - 1):
                     stage_2(i - 1, k)
             if is_step(i - 2):
+                for k in range(TILES):
+                    apply_gain(i - 2, k)
                 reciprocal_rms(i - 2)
-            if is_step(i + 3):
-                transposes(i + 3)
-            if i == -1:
-                regroup_we()
+            if is_step(i + 2):
+                transposes(i + 2)
             if is_step(i):
                 new_cat(i)
                 for piece in range(PIECES):

@@ -23,6 +23,7 @@ STEP_TOKENS = TILES * P
 STEPS = TOKENS // STEP_TOKENS
 PIECES = TILES * STREAMS
 EPS = 1e-6
+LOADS_BEFORE_BROADCASTS = 4
 
 FLOPS = 2 * TOKENS * F * D * STREAMS + 2 * TOKENS * (STREAMS * D) * D
 
@@ -60,6 +61,8 @@ def tile_wavenetworklm_pb_t_kernel(tc, h_r, h_i, w2r, b2r, w2i, b2i, We, be, g_r
             )
             return raw
 
+        be_all = keep.tile([P, D], BF16)
+        gain_all = keep.tile([P, D], BF16)
         w2_raw = [None, None]
         h_tiles = {}
         w2_raw[0] = load_w2(0)
@@ -73,6 +76,9 @@ def tile_wavenetworklm_pb_t_kernel(tc, h_r, h_i, w2r, b2r, w2i, b2i, We, be, g_r
         )
         for n in range(2, STEPS):
             h_tiles[n] = load_h(n)
+            if n == LOADS_BEFORE_BROADCASTS:
+                nc.sync.dma_start(out=be_all[:], in_=be.partition_broadcast(P))
+                nc.sync.dma_start(out=gain_all[:], in_=g_rms.partition_broadcast(P))
 
         identity = keep.tile([P, P], F32)
         make_identity(nc, identity[:])
@@ -84,10 +90,6 @@ def tile_wavenetworklm_pb_t_kernel(tc, h_r, h_i, w2r, b2r, w2i, b2i, We, be, g_r
             b2_sb = keep.tile([P, PACK], BF16, name="b2_%d" % s)
             nc.scalar.dma_start(out=b2_sb[:], in_=b2_dram[s].rearrange("(p t) -> p t", t=PACK))
             b2.append(b2_sb)
-        be_all = keep.tile([P, D], BF16)
-        nc.gpsimd.dma_start(out=be_all[:], in_=be.partition_broadcast(P))
-        gain_all = keep.tile([P, D], BF16)
-        nc.gpsimd.dma_start(out=gain_all[:], in_=g_rms.partition_broadcast(P))
 
         w2_codes = []
         w2_scales = []
@@ -264,13 +266,11 @@ def tile_wavenetworklm_pb_t_kernel(tc, h_r, h_i, w2r, b2r, w2i, b2i, We, be, g_r
         def is_step(n):
             return 0 <= n < STEPS
 
-        for i in range(-2, STEPS + 3):
+        for i in range(-2, STEPS + 2):
             if is_step(i + 1):
                 copy_h(i + 1)
             if i == 0:
                 regroup_we()
-            if is_step(i - 3):
-                norm_second_half(i - 3)
             if is_step(i - 2):
                 new_norm(i - 2)
             for k in range(TILES):
@@ -282,6 +282,7 @@ def tile_wavenetworklm_pb_t_kernel(tc, h_r, h_i, w2r, b2r, w2i, b2i, We, be, g_r
                 for k in range(TILES):
                     apply_gain(i - 2, k)
                 reciprocal_rms(i - 2)
+                norm_second_half(i - 2)
             if is_step(i + 2):
                 transposes(i + 2)
             if is_step(i):

@@ -23,6 +23,7 @@ STEP_TOKENS = TILES * P
 STEPS = TOKENS // STEP_TOKENS
 PIECES = TILES * STREAMS
 EPS = 1e-6
+VECTOR_FINISHES = 2
 LOADS_BEFORE_BROADCASTS = 4
 
 FLOPS = 2 * TOKENS * F * D * STREAMS + 2 * TOKENS * (STREAMS * D) * D
@@ -145,7 +146,6 @@ def tile_wavenetworklm_pb_t_kernel(tc, h_r, h_i, w2r, b2r, w2i, b2i, We, be, g_r
         cat_codes = {}
         sums_2 = {}
         wave = {}
-        gained = {}
         square_sums = {}
         inv_rms = {}
 
@@ -232,10 +232,8 @@ def tile_wavenetworklm_pb_t_kernel(tc, h_r, h_i, w2r, b2r, w2i, b2i, We, be, g_r
 
         def new_norm(n):
             biased = tail.tile([P, TILES, D], F32)
-            with_gain = tail.tile([P, TILES, D], F32)
             totals = tail.tile([P, TILES], F32)
             wave[n] = biased
-            gained[n] = with_gain
             square_sums[n] = totals
 
         def norm_first_half(n, k):
@@ -245,10 +243,6 @@ def tile_wavenetworklm_pb_t_kernel(tc, h_r, h_i, w2r, b2r, w2i, b2i, We, be, g_r
                 out=squares[:], in_=wave[n][:, k, :], func=ACT.Square, accum_out=square_sums[n][:, k : k + 1]
             )
 
-        def apply_gain(n, k):
-            gain_engine = nc.vector if n == STEPS - 1 else nc.gpsimd
-            gain_engine.tensor_tensor(out=gained[n][:, k, :], in0=wave[n][:, k, :], in1=gain_all[:], op=MULT)
-
         def reciprocal_rms(n):
             factors = tail.tile([P, TILES], F32)
             nc.scalar.activation(
@@ -256,12 +250,30 @@ def tile_wavenetworklm_pb_t_kernel(tc, h_r, h_i, w2r, b2r, w2i, b2i, We, be, g_r
             )
             inv_rms[n] = factors
 
-        def norm_second_half(n):
+        def out_rows(n):
+            return out_dram[n * STEP_TOKENS : (n + 1) * STEP_TOKENS, :].rearrange("(p k) d -> p k d", k=TILES)
+
+        def gain_scale_store(n):
+            with_gain = tail.tile([P, TILES, D], F32)
             result = tail.tile([P, TILES, D], F32)
-            rows = out_dram[n * STEP_TOKENS : (n + 1) * STEP_TOKENS, :].rearrange("(p k) d -> p k d", k=TILES)
             for k in range(TILES):
-                nc.scalar.activation(out=result[:, k, :], in_=gained[n][:, k, :], func=ACT.Copy, scale=inv_rms[n][:, k : k + 1])
-                nc.sync.dma_start(out=rows[:, k, :], in_=result[:, k, :])
+                nc.gpsimd.tensor_tensor(out=with_gain[:, k, :], in0=wave[n][:, k, :], in1=gain_all[:], op=MULT)
+            for k in range(TILES):
+                nc.scalar.activation(out=result[:, k, :], in_=with_gain[:, k, :], func=ACT.Copy, scale=inv_rms[n][:, k : k + 1])
+                nc.sync.dma_start(out=out_rows(n)[:, k, :], in_=result[:, k, :])
+
+        def gain_scale_store_on_vector(n):
+            result = tail.tile([P, TILES, D], F32)
+            for k in range(TILES):
+                nc.vector.scalar_tensor_tensor(
+                    out=result[:, k, :],
+                    in0=wave[n][:, k, :],
+                    scalar=inv_rms[n][:, k : k + 1],
+                    in1=gain_all[:],
+                    op0=MULT,
+                    op1=MULT,
+                )
+                nc.sync.dma_start(out=out_rows(n)[:, k, :], in_=result[:, k, :])
 
         def is_step(n):
             return 0 <= n < STEPS
@@ -279,10 +291,9 @@ def tile_wavenetworklm_pb_t_kernel(tc, h_r, h_i, w2r, b2r, w2i, b2i, We, be, g_r
                 if is_step(i - 1):
                     stage_2(i - 1, k)
             if is_step(i - 2):
-                for k in range(TILES):
-                    apply_gain(i - 2, k)
                 reciprocal_rms(i - 2)
-                norm_second_half(i - 2)
+            if is_step(i - 2) and i - 2 < STEPS - VECTOR_FINISHES:
+                gain_scale_store(i - 2)
             if is_step(i + 2):
                 transposes(i + 2)
             if is_step(i):
@@ -297,3 +308,6 @@ def tile_wavenetworklm_pb_t_kernel(tc, h_r, h_i, w2r, b2r, w2i, b2i, We, be, g_r
                 quantise_cat(i)
             if i == 0:
                 quantise_we()
+
+        for n in range(STEPS - VECTOR_FINISHES, STEPS):
+            gain_scale_store_on_vector(n)

from contextlib import ExitStack

import concourse.mybir as mybir
from concourse.masks import make_identity

F32 = mybir.dt.float32
BF16 = mybir.dt.bfloat16
U32 = mybir.dt.uint32
U8 = mybir.dt.uint8
FP8X4 = mybir.dt.float8_e4m3fn_x4
ADD = mybir.AluOpType.add
MULT = mybir.AluOpType.mult
ACT = mybir.ActivationFunctionType

P = 128
PACK = 4
TOKENS = 4096
F = 512
D = 512
STREAMS = 2
TILES = 2
STEP_TOKENS = TILES * P
STEPS = TOKENS // STEP_TOKENS
PIECES = TILES * STREAMS
EPS = 1e-6
VECTOR_FINISHES = 2
LOADS_BEFORE_BROADCASTS = 4

FLOPS = 2 * TOKENS * F * D * STREAMS + 2 * TOKENS * (STREAMS * D) * D


def tile_wavenetworklm_pb_t_kernel(tc, h_r, h_i, w2r, b2r, w2i, b2i, We, be, g_rms, out):
    nc = tc.nc
    h_dram = [h_r.flatten_outer_dims(), h_i.flatten_outer_dims()]
    w2_dram = [w2r, w2i]
    b2_dram = [b2r, b2i]
    out_dram = out.flatten_outer_dims()

    with ExitStack() as stack:
        stack.enter_context(tc.manual_schedule())
        keep = stack.enter_context(tc.tile_pool(name="keep", bufs=1))
        work = stack.enter_context(tc.tile_pool(name="work", bufs=2))
        tail = stack.enter_context(tc.tile_pool(name="tail", bufs=3))
        psum_t = stack.enter_context(tc.psum_pool(name="psum_t", bufs=2))
        psum_1 = stack.enter_context(tc.psum_pool(name="psum_1", bufs=4))
        psum_2 = stack.enter_context(tc.psum_pool(name="psum_2", bufs=2))

        def load_h(n):
            rows = slice(n * STEP_TOKENS, (n + 1) * STEP_TOKENS)
            tiles = []
            for s in range(STREAMS):
                h_sb = keep.tile([P, TILES * F], BF16, name="h_%d_%d" % (s, n))
                nc.sync.dma_start(out=h_sb[:], in_=h_dram[s][rows, :].rearrange("(p k) f -> p (k f)", k=TILES))
                tiles.append(h_sb)
            return tiles

        def load_w2(s):
            raw = keep.tile([P, PACK, D], BF16, name="w2_raw_%d" % s)
            nc.sync.dma_start(
                out=raw[:].rearrange("q (u e) d -> q u (e d)", u=2),
                in_=w2_dram[s].rearrange("(u q e) d -> q u (e d)", u=2, e=2),
            )
            return raw

        be_all = keep.tile([P, D], BF16)
        gain_all = keep.tile([P, D], BF16)
        w2_raw = [None, None]
        h_tiles = {}
        w2_raw[0] = load_w2(0)
        h_tiles[0] = load_h(0)
        w2_raw[1] = load_w2(1)
        h_tiles[1] = load_h(1)
        we_raw = keep.tile([P, STREAMS, PACK, D], BF16)
        nc.sync.dma_start(
            out=we_raw[:].rearrange("p s t d -> p s (t d)"),
            in_=We.rearrange("(s p t) d -> p s (t d)", s=STREAMS, t=PACK),
        )
        for n in range(2, STEPS):
            h_tiles[n] = load_h(n)
            if n == LOADS_BEFORE_BROADCASTS:
                nc.sync.dma_start(out=be_all[:], in_=be.partition_broadcast(P))
                nc.sync.dma_start(out=gain_all[:], in_=g_rms.partition_broadcast(P))

        identity = keep.tile([P, P], F32)
        make_identity(nc, identity[:])
        eps = keep.tile([P, 1], F32)
        nc.vector.memset(eps[:], EPS)

        b2 = []
        for s in range(STREAMS):
            b2_sb = keep.tile([P, PACK], BF16, name="b2_%d" % s)
            nc.scalar.dma_start(out=b2_sb[:], in_=b2_dram[s].rearrange("(p t) -> p t", t=PACK))
            b2.append(b2_sb)

        w2_codes = []
        w2_scales = []

        def prepare_w2(s):
            grouped = keep.tile([P, D * PACK], BF16, name="w2_grouped_%d" % s, align_bytes=64)
            nc.vector.tensor_copy(
                out=grouped[:].rearrange("q (t c j) -> q t c j", t=PACK, j=PACK),
                in_=w2_raw[s][:].rearrange("q j (c t) -> q t c j", t=PACK),
            )
            return grouped

        def quantise_w2(s, grouped):
            codes = keep.tile([P, D], U32, name="w2_codes_%d" % s, align_bytes=64)
            scales = keep.tile([P, D], U8, name="w2_scales_%d" % s, align_bytes=64)
            nc.vector.quantize_mx(out=codes[:].bitcast(FP8X4), scales=scales[:], in_=grouped[:])
            w2_codes.append(codes)
            w2_scales.append(scales)

        for s in range(STREAMS):
            quantise_w2(s, prepare_w2(s))

        we_grouped = keep.tile([P, STREAMS, D * PACK], BF16, align_bytes=64)
        we_codes = keep.tile([P, STREAMS, D], U32, align_bytes=64)
        we_scales = keep.tile([P, STREAMS, D], U8, align_bytes=64)

        def regroup_we():
            nc.scalar.copy(
                out=we_grouped[:, 0, :].rearrange("p (d t) -> p d t", t=PACK),
                in_=we_raw[:, 0, :, :].rearrange("p t d -> p d t"),
            )
            nc.gpsimd.tensor_scalar(
                out=we_grouped[:, 1, :].rearrange("p (d t) -> p d t", t=PACK),
                in0=we_raw[:, 1, :, :].rearrange("p t d -> p d t"),
                scalar1=1.0,
                scalar2=0.0,
                op0=MULT,
                op1=ADD,
            )

        def quantise_we():
            nc.vector.quantize_mx(
                out=we_codes[:].rearrange("p s d -> p (s d)").bitcast(FP8X4),
                scales=we_scales[:].rearrange("p s d -> p (s d)"),
                in_=we_grouped[:].rearrange("p s x -> p (s x)"),
            )

        h_words = {}
        h_grouped = {}
        h_codes = {}
        sums_1 = {}
        cat_grouped = {}
        cat_codes = {}
        sums_2 = {}
        wave = {}
        square_sums = {}
        inv_rms = {}

        def transposes(n):
            for k in range(TILES):
                words = psum_t.tile([P, STREAMS, 2, P], F32)
                for s in range(STREAMS):
                    source = h_tiles[n][s][:].bitcast(F32)
                    for u in range(2):
                        first = k * (F // 2) + u * P
                        nc.tensor.transpose(words[:, s, u, :], source[:, first : first + P], identity[:])
                h_words[(n, k)] = words

        def copy_h(n):
            grouped = work.tile([P, PIECES * P * PACK], BF16, align_bytes=64)
            grouped_words = grouped[:].bitcast(F32)
            width = STREAMS * P * 2
            for k in range(TILES):
                nc.scalar.copy(
                    out=grouped_words[:, k * width : (k + 1) * width].rearrange("p (s r u) -> p s r u", s=STREAMS, u=2),
                    in_=h_words[(n, k)][:].rearrange("p s u r -> p s r u"),
                )
            h_grouped[n] = grouped

        def quantise(grouped, codes_name, scales_name):
            codes = work.tile([P, PIECES * P], U32, name=codes_name, align_bytes=64)
            scales = work.tile([P, PIECES * P], U8, name=scales_name, align_bytes=64)
            nc.vector.quantize_mx(out=codes[:].bitcast(FP8X4), scales=scales[:], in_=grouped[:])
            return codes, scales

        def quantise_h(n):
            h_codes[n] = quantise(h_grouped[n], "h_codes", "h_scales")

        def stage_1(n, piece):
            s = piece % STREAMS
            codes, scales = h_codes[n]
            tokens = slice(piece * P, (piece + 1) * P)
            sums = psum_1.tile([P, PACK, P], F32)
            for t in range(PACK):
                columns = slice(t * P, (t + 1) * P)
                nc.tensor.matmul_mx(
                    out=sums[:, t, :],
                    lhsT=w2_codes[s][:, columns].bitcast(FP8X4),
                    lhsT_scale=w2_scales[s][:, columns],
                    rhs=codes[:, tokens].bitcast(FP8X4),
                    rhs_scale=scales[:, tokens],
                    start=True,
                    stop=True,
                )
            sums_1[(n, piece)] = sums

        def new_cat(n):
            cat = work.tile([P, PIECES * P * PACK], BF16, align_bytes=64)
            cat_grouped[n] = cat

        def bias_and_round(n, piece):
            s = piece % STREAMS
            width = P * PACK
            nc.vector.tensor_tensor(
                out=cat_grouped[n][:, piece * width : (piece + 1) * width].rearrange("p (r t) -> p r t", t=PACK),
                in0=sums_1[(n, piece)][:].rearrange("p t r -> p r t"),
                in1=b2[s][:].unsqueeze(1).to_broadcast([P, P, PACK]),
                op=ADD,
            )

        def quantise_cat(n):
            cat_codes[n] = quantise(cat_grouped[n], "cat_codes", "cat_scales")

        def stage_2(n, k):
            codes, scales = cat_codes[n]
            sums = psum_2.tile([P, D], F32)
            for s in range(STREAMS):
                tokens = slice((k * STREAMS + s) * P, (k * STREAMS + s + 1) * P)
                nc.tensor.matmul_mx(
                    out=sums[:],
                    lhsT=codes[:, tokens].bitcast(FP8X4),
                    lhsT_scale=scales[:, tokens],
                    rhs=we_codes[:, s, :].bitcast(FP8X4),
                    rhs_scale=we_scales[:, s, :],
                    start=(s == 0),
                    stop=(s == STREAMS - 1),
                )
            sums_2[(n, k)] = sums

        def new_norm(n):
            biased = tail.tile([P, TILES, D], F32)
            totals = tail.tile([P, TILES], F32)
            wave[n] = biased
            square_sums[n] = totals

        def norm_first_half(n, k):
            nc.vector.tensor_tensor(out=wave[n][:, k, :], in0=sums_2[(n, k)][:], in1=be_all[:], op=ADD)
            squares = work.tile([P, D], BF16)
            nc.scalar.activation(
                out=squares[:], in_=wave[n][:, k, :], func=ACT.Square, accum_out=square_sums[n][:, k : k + 1]
            )

        def reciprocal_rms(n):
            factors = tail.tile([P, TILES], F32)
            nc.scalar.activation(
                out=factors[:], in_=square_sums[n][:], func=ACT.Abs_reciprocal_sqrt, scale=1.0 / D, bias=eps[:]
            )
            inv_rms[n] = factors

        def out_rows(n):
            return out_dram[n * STEP_TOKENS : (n + 1) * STEP_TOKENS, :].rearrange("(p k) d -> p k d", k=TILES)

        def gain_scale_store(n):
            with_gain = tail.tile([P, TILES, D], F32)
            result = tail.tile([P, TILES, D], F32)
            for k in range(TILES):
                nc.gpsimd.tensor_tensor(out=with_gain[:, k, :], in0=wave[n][:, k, :], in1=gain_all[:], op=MULT)
            for k in range(TILES):
                nc.scalar.activation(out=result[:, k, :], in_=with_gain[:, k, :], func=ACT.Copy, scale=inv_rms[n][:, k : k + 1])
                nc.sync.dma_start(out=out_rows(n)[:, k, :], in_=result[:, k, :])

        def gain_scale_store_on_vector(n):
            result = tail.tile([P, TILES, D], F32)
            for k in range(TILES):
                nc.vector.scalar_tensor_tensor(
                    out=result[:, k, :],
                    in0=wave[n][:, k, :],
                    scalar=inv_rms[n][:, k : k + 1],
                    in1=gain_all[:],
                    op0=MULT,
                    op1=MULT,
                )
                nc.sync.dma_start(out=out_rows(n)[:, k, :], in_=result[:, k, :])

        def is_step(n):
            return 0 <= n < STEPS

        for i in range(-2, STEPS + 2):
            if is_step(i + 1):
                copy_h(i + 1)
            if i == 0:
                regroup_we()
            if is_step(i - 2):
                new_norm(i - 2)
            for k in range(TILES):
                if is_step(i - 2):
                    norm_first_half(i - 2, k)
                if is_step(i - 1):
                    stage_2(i - 1, k)
            if is_step(i - 2):
                reciprocal_rms(i - 2)
            if is_step(i - 2) and i - 2 < STEPS - VECTOR_FINISHES:
                gain_scale_store(i - 2)
            if is_step(i + 2):
                transposes(i + 2)
            if is_step(i):
                new_cat(i)
                for piece in range(PIECES):
                    bias_and_round(i, piece)
            if is_step(i + 1):
                quantise_h(i + 1)
                for piece in range(PIECES):
                    stage_1(i + 1, piece)
            if is_step(i):
                quantise_cat(i)
            if i == 0:
                quantise_we()

        for n in range(STEPS - VECTOR_FINISHES, STEPS):
            gain_scale_store_on_vector(n)
